import numpy as np
import ml_dtypes

BF16 = ml_dtypes.bfloat16


def bf(x):
    return np.asarray(x, np.float32).astype(BF16)


def f32(x):
    return np.asarray(x, np.float32)


def f64(x):
    return np.asarray(x).astype(np.float64)


def striped(idx):
    return np.tile(idx.reshape(-1, 16).T, (8, 1))


C, S, N, K = 128, 256, 64, 16


def setup_inputs():
    t = np.random.random((C, N, K)).argmax(axis=-1)
    return {"base": f32(np.random.standard_normal((C, S))), "pred_probs": f32(0.05 + 0.95 * np.random.random((C, N, K))), "sel": f32(np.eye(K)[t]), "mask": f32(0.5 + np.random.random((C, N))), "offs": striped(np.random.permutation(S)[:N])}


def reference(base, pred_probs, sel, mask, offs):
    idx = offs[:16].T.reshape(-1)
    nll = -np.sum(f64(sel) * np.log(f64(pred_probs)), axis=-1)
    out = f64(base).copy()
    out[:, idx] = nll * f64(mask)
    return out

@@ -1,0 +1,39 @@
+import concourse.mybir as mybir
+
+F32 = mybir.dt.float32
+U16 = mybir.dt.uint16
+LN = mybir.ActivationFunctionType.Ln
+MULT = mybir.AluOpType.mult
+ADD = mybir.AluOpType.add
+INNERMOST = mybir.AxisListType.X
+
+C = 128
+S = 256
+N = 64
+K = 16
+
+
+def tile_ordinalcrossentropyloss_kernel(tc, base, pred_probs, sel, mask, offs, out):
+    nc = tc.nc
+    with tc.tile_pool(name="held", bufs=1) as held:
+        offsets = held.tile([C, N // 16], U16, name="offsets")
+        nc.sync.dma_start(offsets[:], offs)
+
+        probs = held.tile([C, N, K], F32, name="probs")
+        nc.sync.dma_start(probs[:], pred_probs)
+        target = held.tile([C, N, K], F32, name="target")
+        nc.scalar.dma_start(target[:], sel)
+        weight = held.tile([C, N], F32, name="weight")
+        nc.sync.dma_start(weight[:], mask)
+        loss_map = held.tile([C, S], F32, name="loss_map")
+        nc.scalar.dma_start(loss_map[:], base)
+
+        log_probs = held.tile([C, N, K], F32, name="log_probs")
+        nc.scalar.activation(log_probs[:], probs[:], LN)
+        picked = held.tile([C, N, K], F32, name="picked")
+        nc.vector.tensor_tensor(picked[:], target[:], log_probs[:], MULT)
+        nll = held.tile([C, N], F32, name="nll")
+        nc.vector.tensor_reduce(nll[:], picked[:], axis=INNERMOST, op=ADD, negate=True)
+
+        nc.vector.tensor_tensor(loss_map[:].indirect(offsets[:]), nll[:], weight[:], MULT)
+        nc.sync.dma_start(out, loss_map[:])

@@ -12,6 +12,9 @@ S = 256
 N = 64
 K = 16
 
+CHUNKS = 4
+J = N // CHUNKS
+
 
 def tile_ordinalcrossentropyloss_kernel(tc, base, pred_probs, sel, mask, offs, out):
     nc = tc.nc
@@ -19,21 +22,25 @@ def tile_ordinalcrossentropyloss_kernel(tc, base, pred_probs, sel, mask, offs, o
         offsets = held.tile([C, N // 16], U16, name="offsets")
         nc.sync.dma_start(offsets[:], offs)
 
-        probs = held.tile([C, N, K], F32, name="probs")
-        nc.sync.dma_start(probs[:], pred_probs)
-        target = held.tile([C, N, K], F32, name="target")
-        nc.scalar.dma_start(target[:], sel)
+        probs = [held.tile([C, J, K], F32, name=f"probs{i}") for i in range(CHUNKS)]
+        target = [held.tile([C, J, K], F32, name=f"target{i}") for i in range(CHUNKS)]
+        for i in range(CHUNKS):
+            nc.sync.dma_start(probs[i][:], pred_probs[:, i * J : (i + 1) * J, :])
+            nc.scalar.dma_start(target[i][:], sel[:, i * J : (i + 1) * J, :])
         weight = held.tile([C, N], F32, name="weight")
         nc.sync.dma_start(weight[:], mask)
         loss_map = held.tile([C, S], F32, name="loss_map")
-        nc.scalar.dma_start(loss_map[:], base)
+        nc.sync.dma_start(loss_map[:], base)
 
-        log_probs = held.tile([C, N, K], F32, name="log_probs")
-        nc.scalar.activation(log_probs[:], probs[:], LN)
-        picked = held.tile([C, N, K], F32, name="picked")
-        nc.vector.tensor_tensor(picked[:], target[:], log_probs[:], MULT)
         nll = held.tile([C, N], F32, name="nll")
-        nc.vector.tensor_reduce(nll[:], picked[:], axis=INNERMOST, op=ADD, negate=True)
+        for i in range(CHUNKS):
+            log_probs = held.tile([C, J, K], F32, name=f"log_probs{i}")
+            nc.scalar.activation(log_probs[:], probs[i][:], LN)
+            picked = held.tile([C, J, K], F32, name=f"picked{i}")
+            nc.vector.tensor_tensor(picked[:], target[i][:], log_probs[:], MULT)
+            nc.vector.tensor_reduce(
+                nll[:, i * J : (i + 1) * J], picked[:], axis=INNERMOST, op=ADD, negate=True
+            )
 
         nc.vector.tensor_tensor(loss_map[:].indirect(offsets[:]), nll[:], weight[:], MULT)
         nc.sync.dma_start(out, loss_map[:])

@@ -12,34 +12,42 @@ S = 256
 N = 64
 K = 16
 
-CHUNKS = 4
-J = N // CHUNKS
+CHUNK = 16
+PAIR = 2 * CHUNK
 
 
 def tile_ordinalcrossentropyloss_kernel(tc, base, pred_probs, sel, mask, offs, out):
     nc = tc.nc
     with tc.tile_pool(name="held", bufs=1) as held:
+        probs = held.tile([C, N, K], F32, name="probs")
+        target = held.tile([C, N, K], F32, name="target")
+        weight = held.tile([C, N], F32, name="weight")
+        loss_map = held.tile([C, S], F32, name="loss_map")
         offsets = held.tile([C, N // 16], U16, name="offsets")
+
+        for first in range(0, N, PAIR):
+            nc.sync.dma_start(
+                probs[:, first : first + PAIR, :], pred_probs[:, first : first + PAIR, :]
+            )
+            for start in range(first, first + PAIR, CHUNK):
+                nc.sync.dma_start(
+                    target[:, start : start + CHUNK, :], sel[:, start : start + CHUNK, :]
+                )
+        nc.sync.dma_start(weight[:], mask)
+        nc.sync.dma_start(loss_map[:], base)
         nc.sync.dma_start(offsets[:], offs)
 
-        probs = [held.tile([C, J, K], F32, name=f"probs{i}") for i in range(CHUNKS)]
-        target = [held.tile([C, J, K], F32, name=f"target{i}") for i in range(CHUNKS)]
-        for i in range(CHUNKS):
-            nc.sync.dma_start(probs[i][:], pred_probs[:, i * J : (i + 1) * J, :])
-            nc.scalar.dma_start(target[i][:], sel[:, i * J : (i + 1) * J, :])
-        weight = held.tile([C, N], F32, name="weight")
-        nc.sync.dma_start(weight[:], mask)
-        loss_map = held.tile([C, S], F32, name="loss_map")
-        nc.sync.dma_start(loss_map[:], base)
-
+        log_probs = held.tile([C, N, K], F32, name="log_probs")
+        picked = held.tile([C, N, K], F32, name="picked")
         nll = held.tile([C, N], F32, name="nll")
-        for i in range(CHUNKS):
-            log_probs = held.tile([C, J, K], F32, name=f"log_probs{i}")
-            nc.scalar.activation(log_probs[:], probs[i][:], LN)
-            picked = held.tile([C, J, K], F32, name=f"picked{i}")
-            nc.vector.tensor_tensor(picked[:], target[i][:], log_probs[:], MULT)
+        for start in range(0, N, CHUNK):
+            chunk = slice(start, start + CHUNK)
+            nc.scalar.activation(log_probs[:, chunk, :], probs[:, chunk, :], LN)
+            nc.vector.tensor_tensor(
+                picked[:, chunk, :], target[:, chunk, :], log_probs[:, chunk, :], MULT
+            )
             nc.vector.tensor_reduce(
-                nll[:, i * J : (i + 1) * J], picked[:], axis=INNERMOST, op=ADD, negate=True
+                nll[:, chunk], picked[:, chunk, :], axis=INNERMOST, op=ADD, negate=True
             )
 
         nc.vector.tensor_tensor(loss_map[:].indirect(offsets[:]), nll[:], weight[:], MULT)

@@ -29,10 +29,9 @@ def tile_ordinalcrossentropyloss_kernel(tc, base, pred_probs, sel, mask, offs, o
             nc.sync.dma_start(
                 probs[:, first : first + PAIR, :], pred_probs[:, first : first + PAIR, :]
             )
-            for start in range(first, first + PAIR, CHUNK):
-                nc.sync.dma_start(
-                    target[:, start : start + CHUNK, :], sel[:, start : start + CHUNK, :]
-                )
+            nc.sync.dma_start(
+                target[:, first : first + PAIR, :], sel[:, first : first + PAIR, :]
+            )
         nc.sync.dma_start(weight[:], mask)
         nc.sync.dma_start(loss_map[:], base)
         nc.sync.dma_start(offsets[:], offs)

import concourse.mybir as mybir

F32 = mybir.dt.float32
U16 = mybir.dt.uint16
LN = mybir.ActivationFunctionType.Ln
MULT = mybir.AluOpType.mult
ADD = mybir.AluOpType.add
INNERMOST = mybir.AxisListType.X

C = 128
S = 256
N = 64
K = 16

CHUNK = 16
PAIR = 2 * CHUNK


def tile_ordinalcrossentropyloss_kernel(tc, base, pred_probs, sel, mask, offs, out):
    nc = tc.nc
    with tc.tile_pool(name="held", bufs=1) as held:
        probs = held.tile([C, N, K], F32, name="probs")
        target = held.tile([C, N, K], F32, name="target")
        weight = held.tile([C, N], F32, name="weight")
        loss_map = held.tile([C, S], F32, name="loss_map")
        offsets = held.tile([C, N // 16], U16, name="offsets")

        for first in range(0, N, PAIR):
            nc.sync.dma_start(
                probs[:, first : first + PAIR, :], pred_probs[:, first : first + PAIR, :]
            )
            nc.sync.dma_start(
                target[:, first : first + PAIR, :], sel[:, first : first + PAIR, :]
            )
        nc.sync.dma_start(weight[:], mask)
        nc.sync.dma_start(loss_map[:], base)
        nc.sync.dma_start(offsets[:], offs)

        log_probs = held.tile([C, N, K], F32, name="log_probs")
        picked = held.tile([C, N, K], F32, name="picked")
        nll = held.tile([C, N], F32, name="nll")
        for start in range(0, N, CHUNK):
            chunk = slice(start, start + CHUNK)
            nc.scalar.activation(log_probs[:, chunk, :], probs[:, chunk, :], LN)
            nc.vector.tensor_tensor(
                picked[:, chunk, :], target[:, chunk, :], log_probs[:, chunk, :], MULT
            )
            nc.vector.tensor_reduce(
                nll[:, chunk], picked[:, chunk, :], axis=INNERMOST, op=ADD, negate=True
            )

        nc.vector.tensor_tensor(loss_map[:].indirect(offsets[:]), nll[:], weight[:], MULT)
        nc.sync.dma_start(out, loss_map[:])
